import numpy as np
import ml_dtypes


def mxq(x, axis, fmt="e4m3"):
    dtype, down = {"e4m3": (ml_dtypes.float8_e4m3fn, 7), "e5m2": (ml_dtypes.float8_e5m2, 14)}[fmt]
    v = np.moveaxis(np.asarray(x, np.float32).astype(ml_dtypes.bfloat16).astype(np.float64), axis, -1)
    blocks = v.reshape(v.shape[:-1] + (-1, 32))
    amax = np.abs(blocks).max(-1, keepdims=True)
    byte = np.maximum(np.where(amax > 0, np.frexp(amax)[1] - 1 + 127, 0) - down, 1)
    scale = np.exp2(byte - 127.0)
    codes = (blocks / scale).astype(np.float32).astype(dtype).astype(np.float64)
    return np.moveaxis((codes * scale).reshape(v.shape), -1, axis)


WIDE = False


def mx_kscale(k):
    if not WIDE:
        return np.ones(k)
    levels = np.array([18, -18])
    if k % 512:
        return np.exp2(np.random.permutation(np.resize(levels, k // 32))).repeat(32)
    a = np.empty((k // 512, 16))
    for p in range(k // 512):
        a[p, :8] = np.random.permutation(np.resize(levels, 8))
        for g in range(8):
            far = levels[np.abs(levels - a[p, g]) >= 10]
            a[p, g + 8] = far[np.random.randint(len(far))]
    return np.exp2(a.ravel()).repeat(32)


BF16 = ml_dtypes.bfloat16


def bf(x):
    return np.asarray(x, np.float32).astype(BF16)


def f64(x):
    return np.asarray(x).astype(np.float64)


B, L0, L1, L2, L3 = 1024, 1024, 512, 512, 512
DT = 1.0
TAU_J = 10.0
TAU_M = 20.0
KAPPA_J = 0.25
THRESH = 0.4
X_DECAY = 20.0
P_FIRE = 0.2


def current_and_membrane(e_gen2, e_disc2, e_gen1, e_disc3, j2, v2, Eg1, Ed2):
    total = (-(f64(e_gen2) + f64(e_disc2))
             + f64(e_gen1) @ f64(Eg1).T
             + f64(e_disc3) @ f64(Ed2).T)
    j = f64(j2) + (DT / TAU_J) * (-KAPPA_J * f64(j2) + total)
    v = f64(v2) + (DT / TAU_M) * (-f64(v2) + j)
    return j, v


def setup_inputs():
    s = mx_kscale(B)[:, None]
    u = mx_kscale(L2)
    e_gen2 = bf(np.random.random((B, L2)) * 2.0 + np.random.standard_normal((B, L2)) * 0.7)
    e_disc2 = bf(np.random.random((B, L2)) * 2.0 + np.random.standard_normal((B, L2)) * 0.7)
    e_gen1_0 = bf(np.random.random((B, L1)) * 2.0 + np.random.standard_normal((B, L1)) * 0.7)
    e_disc3 = bf((np.random.random((B, L3)) < P_FIRE) + np.random.standard_normal((B, L3)) * 0.7)
    j2 = bf(np.random.standard_normal((B, L2)) * 1.5)
    v2 = bf(np.random.standard_normal((B, L2)) * 0.4)
    x2 = bf(np.random.random((B, L2)) * 2.0)
    Eg1_0 = bf(np.random.standard_normal((L2, L1)) * 2.0 / np.sqrt(L1))
    Ed2 = bf(np.random.standard_normal((L2, L3)) * 2.0 / np.sqrt(L3))
    _, v = current_and_membrane(e_gen2, e_disc2, e_gen1_0, e_disc3, j2, v2, Eg1_0, Ed2)
    side = np.where(v > THRESH, 1.0, -1.0)
    v2 = bf(f64(v2) + np.where(np.abs(v - THRESH) < 0.02, 0.05 * side, 0.0))
    _, v = current_and_membrane(e_gen2, e_disc2, e_gen1_0, e_disc3, j2, v2, Eg1_0, Ed2)
    cols = np.repeat(np.array([1.0, 16.0, 1.0, 1.0]), L2)
    g = bf(np.random.standard_normal((B, 4 * L2)) * np.exp2(np.random.randint(-6, 1, (B, 1))) * 4.0 * cols
           / s * np.tile(u, 4))
    return {
        "e_gen2": e_gen2,
        "e_disc2": e_disc2,
        "e_gen1": bf(f64(e_gen1_0) * s),
        "e_disc3": e_disc3,
        "j2": j2,
        "v2": v2,
        "x2": x2,
        "Eg1": bf(f64(Eg1_0) / u[:, None]),
        "Ed2": Ed2,
        "v_pre": np.asarray(v, np.float32),
        "grad_out": g,
    }


def reference(e_gen2, e_disc2, e_gen1, e_disc3, j2, v2, x2, Eg1, Ed2, v_pre, grad_out):
    g = f64(grad_out)
    gj = g[:, :L2]
    gv = g[:, L2:2 * L2]
    keep = np.where(f64(v_pre) > THRESH, 0.0, 1.0)
    dz = (DT / TAU_J) * (gj + (DT / TAU_M) * keep * gv)
    dx = mxq(dz, 1, "e5m2") @ mxq(f64(Eg1), 0, "e4m3")
    dw = mxq(dz, 0, "e5m2").T @ mxq(f64(e_gen1), 0, "e4m3")
    return dx, dw

@@ -1,0 +1,262 @@
+from contextlib import ExitStack
+
+import concourse.mybir as mybir
+from concourse.masks import make_identity
+
+F32 = mybir.dt.float32
+BF16 = mybir.dt.bfloat16
+U32 = mybir.dt.uint32
+U8 = mybir.dt.uint8
+E4M3 = mybir.dt.float8_e4m3fn_x4
+E5M2 = mybir.dt.float8_e5m2_x4
+OP = mybir.AluOpType
+COPY = mybir.ActivationFunctionType.Copy
+
+P = 128
+PACK = 4
+N = 512
+TOKENS = 1024
+FLOPS = 2 * 2 * TOKENS * N * N
+BYTES = TOKENS * N * (4 + 2 + 2 + 2) + N * N * 2 + TOKENS * N * 4 + N * N * 4
+
+
+def tile_bspncn_pb_v_kernel(tc, e_gen2, e_disc2, e_gen1, e_disc3, j2, v2, x2, Eg1, Ed2, v_pre, grad_out, out_0, out_1):
+    nc = tc.nc
+    v_hbm = v_pre.rearrange("(g p j) w -> g p j w", p=P, j=PACK)
+    g_hbm = grad_out.rearrange("(g p j) w -> g p j w", p=P, j=PACK)
+    e_hbm = e_gen1.rearrange("(g p j) w -> g p j w", p=P, j=PACK)
+    eg_hbm = Eg1.rearrange("(p j) w -> p j w", j=PACK)
+    o0_hbm = out_0.rearrange("(g p j) w -> g p j w", p=P, j=PACK)
+
+    with ExitStack() as ctx:
+        keep = ctx.enter_context(tc.tile_pool(name="keep", bufs=1))
+        t_psum = ctx.enter_context(tc.psum_pool(name="t_psum", bufs=2))
+        o0_psum = ctx.enter_context(tc.psum_pool(name="o0_psum", bufs=2))
+        o1_psum = ctx.enter_context(tc.psum_pool(name="o1_psum", bufs=1))
+
+        def sb(name, shape, dtype):
+            return keep.tile(shape, dtype, name=name, align_bytes=64)
+
+        ident = sb("ident", [P, P], F32)
+        v_t = [sb(f"v{i}", [P, 2, N], F32) for i in range(4)]
+        g_t = [sb(f"g{i}", [P, 2, 2 * N], BF16) for i in range(4)]
+        e_raw = [sb(f"e{g}", [P, PACK, N], BF16) for g in range(2)]
+        eg_raw = sb("eg", [P, PACK, N], BF16)
+        m_t = [sb(f"m{k}", [P, N], BF16) for k in range(8)]
+        s_t = [sb(f"s{g}", [P, PACK, N], F32) for g in range(2)]
+        d_t = [sb(f"d{g}", [P, N, PACK], BF16) for g in range(2)]
+        e_t = [sb(f"ei{g}", [P, N, PACK], BF16) for g in range(2)]
+        eg_t = sb("egi", [P, N, PACK], BF16)
+        x_t = [sb(f"x{i}", [P, 2, P, PACK], BF16) for i in range(4)]
+        dc = [sb(f"dc{g}", [P, N], U32) for g in range(2)]
+        dsc = [sb(f"ds{g}", [P, N], U8) for g in range(2)]
+        ec = [sb(f"ec{g}", [P, N], U32) for g in range(2)]
+        esc = [sb(f"es{g}", [P, N], U8) for g in range(2)]
+        egc = sb("egc", [P, N], U32)
+        egs = sb("egs", [P, N], U8)
+        xc = [sb(f"xc{i}", [P, 2 * P], U32) for i in range(4)]
+        xs = [sb(f"xs{i}", [P, 2 * P], U8) for i in range(4)]
+        r0 = [sb(f"r0{i}", [P, 2, N], F32) for i in range(4)]
+        r1 = [sb(f"r1{t}", [P, N], F32) for t in range(4)]
+
+        def load_v(i, a, b):
+            nc.sync.dma_start(out=v_t[i][:, a:b, :], in_=v_hbm[i // 2][:, 2 * (i % 2) + a:2 * (i % 2) + b, :])
+
+        def load_g(i, a, b):
+            nc.sync.dma_start(out=g_t[i][:, a:b, :], in_=g_hbm[i // 2][:, 2 * (i % 2) + a:2 * (i % 2) + b, 0:2 * N])
+
+        def load_g_half(i, c0):
+            nc.sync.dma_start(out=g_t[i][:, :, c0:c0 + N], in_=g_hbm[i // 2][:, 2 * (i % 2):2 * (i % 2) + 2, c0:c0 + N])
+
+        def load_e(g):
+            nc.sync.dma_start(out=e_raw[g][:], in_=e_hbm[g])
+
+        def copy(eng, out, in_):
+            if eng == "V":
+                nc.vector.tensor_copy(out=out, in_=in_)
+            else:
+                nc.scalar.copy(out=out, in_=in_)
+
+        def inter(eng, dst, src, h):
+            c = slice(256 * h, 256 * h + 256)
+            copy(eng, dst[:, c, :], src[:, :, c].rearrange("p j w -> p w j"))
+
+        def scale_round(eng, out, in_):
+            if eng == "V":
+                nc.vector.tensor_scalar(out=out, in0=in_, scalar1=0.1, scalar2=None, op0=OP.mult)
+            else:
+                nc.scalar.activation(out=out, in_=in_, func=COPY, scale=0.1)
+
+        def d_inter(eng, g, h):
+            c = slice(256 * h, 256 * h + 256)
+            scale_round(eng, d_t[g][:, c, :], s_t[g][:, :, c].rearrange("p j w -> p w j"))
+
+        def quant(dst, sc, src, c0, w, fmt):
+            nc.vector.quantize_mx(out=dst[:, c0:c0 + w].bitcast(fmt), scales=sc[:, c0:c0 + w],
+                                  in_=src[:, c0:c0 + w, :].rearrange("p w j -> p (w j)"))
+
+        def op1(k):
+            i, jj = divmod(k, 2)
+            nc.vector.scalar_tensor_tensor(out=m_t[k][:], in0=v_t[i][:, jj, :], scalar=0.4,
+                                           in1=g_t[i][:, jj, N:2 * N], op0=OP.is_le, op1=OP.mult)
+
+        def op2(k):
+            i, jj = divmod(k, 2)
+            nc.vector.scalar_tensor_tensor(out=s_t[k // 4][:, k % 4, :], in0=m_t[k][:], scalar=0.05,
+                                           in1=g_t[i][:, jj, 0:N], op0=OP.mult, op1=OP.add)
+
+        tps = {}
+
+        def tr(k):
+            tp = t_psum.tile([P, PACK, P], F32, name="tp")
+            tps[k] = tp
+            for t in range(PACK):
+                nc.tensor.transpose(tp[:, t, :], s_t[k // 4][:, k % 4, t::PACK], ident[:])
+
+        def tcopy(eng, k):
+            scale_round(eng, x_t[k // 2][:, k % 2, :, :], tps[k][:].rearrange("q t p -> q p t"))
+
+        def tq(i):
+            nc.vector.quantize_mx(out=xc[i][:].bitcast(E5M2), scales=xs[i][:],
+                                  in_=x_t[i][:].rearrange("q j p t -> q (j p t)"))
+
+        o0s = {}
+
+        def mm0(k):
+            i, jj = divmod(k, 2)
+            op = o0_psum.tile([P, N], F32, name="o0p")
+            o0s[k] = op
+            c = slice(P * jj, P * jj + P)
+            nc.tensor.matmul_mx(out=op[:], lhsT=xc[i][:, c].bitcast(E5M2), lhsT_scale=xs[i][:, c],
+                                rhs=egc[:].bitcast(E4M3), rhs_scale=egs[:], start=True, stop=True)
+
+        def oc0(eng, k):
+            copy(eng, r0[k // 2][:, k % 2, :], o0s[k][:])
+
+        def st0(k):
+            nc.sync.dma_start(out=o0_hbm[k // 4][:, k % 4, :], in_=r0[k // 2][:, k % 2, :])
+
+        o1 = [o1_psum.tile([P, N], F32, name=f"o1p{t}") for t in range(4)]
+
+        def mm1(g, t):
+            c = slice(P * t, P * t + P)
+            nc.tensor.matmul_mx(out=o1[t][:], lhsT=dc[g][:, c].bitcast(E5M2), lhsT_scale=dsc[g][:, c],
+                                rhs=ec[g][:].bitcast(E4M3), rhs_scale=esc[g][:], start=(g == 0), stop=(g == 1))
+
+        def oc1(eng, t):
+            copy(eng, r1[t][:], o1[t][:])
+
+        def st1(t):
+            nc.sync.dma_start(out=out_1[P * t:P * t + P, :], in_=r1[t][:])
+
+        make_identity(nc, ident[:])
+        with tc.manual_schedule():
+            load_g_half(0, N)
+            load_v(0, 0, 1)
+            load_v(0, 1, 2)
+            load_g_half(0, 0)
+            load_v(1, 0, 2)
+            load_g(1, 0, 2)
+            nc.sync.dma_start(out=eg_raw[:], in_=eg_hbm)
+            load_e(0)
+            load_g(2, 0, 2)
+            load_v(2, 0, 2)
+            load_g(3, 0, 2)
+            load_v(3, 0, 2)
+            load_e(1)
+
+            op1(0)
+            op1(1)
+            op2(0)
+            tr(0)
+            op2(1)
+            tr(1)
+            tcopy("S", 0)
+            tcopy("S", 1)
+            inter("S", eg_t, eg_raw, 0)
+            inter("S", eg_t, eg_raw, 1)
+            op1(2)
+            op1(3)
+            op2(2)
+            tr(2)
+            op2(3)
+            tr(3)
+            d_inter("S", 0, 0)
+            tcopy("S", 2)
+            tcopy("S", 3)
+            tq(0)
+            inter("V", e_t[0], e_raw[0], 0)
+            quant(egc, egs, eg_t, 0, N, E4M3)
+            mm0(0)
+            mm0(1)
+            oc0("S", 0)
+            st0(0)
+            oc0("S", 1)
+            st0(1)
+            op1(4)
+            op1(5)
+            op2(4)
+            tr(4)
+            tq(1)
+            op2(5)
+            tr(5)
+            mm0(2)
+            mm0(3)
+            tcopy("S", 4)
+            inter("S", e_t[0], e_raw[0], 1)
+            tcopy("S", 5)
+            op1(6)
+            quant(dc[0], dsc[0], d_t[0], 0, 256, E5M2)
+            op1(7)
+            op2(6)
+            tr(6)
+            quant(ec[0], esc[0], e_t[0], 0, 256, E4M3)
+            op2(7)
+            tr(7)
+            tq(2)
+            mm0(4)
+            quant(ec[0], esc[0], e_t[0], 256, 256, E4M3)
+            mm1(0, 0)
+            mm1(0, 1)
+            oc0("S", 2)
+            st0(2)
+            oc0("S", 3)
+            st0(3)
+            inter("S", e_t[1], e_raw[1], 0)
+            d_inter("V", 1, 0)
+            inter("V", e_t[1], e_raw[1], 1)
+            tcopy("S", 6)
+            mm0(5)
+            quant(dc[1], dsc[1], d_t[1], 0, 256, E5M2)
+            tcopy("S", 7)
+            oc0("S", 4)
+            st0(4)
+            oc0("S", 5)
+            st0(5)
+            quant(ec[1], esc[1], e_t[1], 256, 256, E4M3)
+            quant(ec[1], esc[1], e_t[1], 0, 256, E4M3)
+            mm1(1, 0)
+            mm1(1, 1)
+            d_inter("V", 0, 1)
+            tq(3)
+            mm0(6)
+            mm0(7)
+            oc1("S", 0)
+            st1(0)
+            d_inter("V", 1, 1)
+            oc0("S", 6)
+            st0(6)
+            oc0("S", 7)
+            st0(7)
+            quant(dc[0], dsc[0], d_t[0], 256, 256, E5M2)
+            quant(dc[1], dsc[1], d_t[1], 256, 256, E5M2)
+            mm1(0, 2)
+            mm1(1, 2)
+            mm1(0, 3)
+            mm1(1, 3)
+            oc1("V", 1)
+            st1(1)
+            oc1("S", 2)
+            st1(2)
+            oc1("V", 3)
+            st1(3)

@@ -77,9 +77,15 @@ def tile_bspncn_pb_v_kernel(tc, e_gen2, e_disc2, e_gen1, e_disc3, j2, v2, x2, Eg
             else:
                 nc.scalar.copy(out=out, in_=in_)
 
+        def four_by_four_in(ap):
+            return ap.rearrange("p j (c i) -> p c j i", i=4)
+
+        def four_by_four_out(ap):
+            return ap.rearrange("p (c i) j -> p c j i", i=4)
+
         def inter(eng, dst, src, h):
             c = slice(256 * h, 256 * h + 256)
-            copy(eng, dst[:, c, :], src[:, :, c].rearrange("p j w -> p w j"))
+            copy(eng, four_by_four_out(dst[:, c, :]), four_by_four_in(src[:, :, c]))
 
         def scale_round(eng, out, in_):
             if eng == "V":
@@ -89,7 +95,7 @@ def tile_bspncn_pb_v_kernel(tc, e_gen2, e_disc2, e_gen1, e_disc3, j2, v2, x2, Eg
 
         def d_inter(eng, g, h):
             c = slice(256 * h, 256 * h + 256)
-            scale_round(eng, d_t[g][:, c, :], s_t[g][:, :, c].rearrange("p j w -> p w j"))
+            scale_round(eng, four_by_four_out(d_t[g][:, c, :]), four_by_four_in(s_t[g][:, :, c]))
 
         def quant(dst, sc, src, c0, w, fmt):
             nc.vector.quantize_mx(out=dst[:, c0:c0 + w].bitcast(fmt), scales=sc[:, c0:c0 + w],
@@ -155,108 +161,107 @@ def tile_bspncn_pb_v_kernel(tc, e_gen2, e_disc2, e_gen1, e_disc3, j2, v2, x2, Eg
             load_v(0, 0, 1)
             load_v(0, 1, 2)
             load_g_half(0, 0)
-            load_v(1, 0, 2)
-            load_g(1, 0, 2)
-            nc.sync.dma_start(out=eg_raw[:], in_=eg_hbm)
             load_e(0)
+            load_g(1, 0, 2)
+            load_v(1, 0, 2)
+            nc.sync.dma_start(out=eg_raw[:], in_=eg_hbm)
             load_g(2, 0, 2)
             load_v(2, 0, 2)
-            load_g(3, 0, 2)
             load_v(3, 0, 2)
             load_e(1)
-
+            load_g(3, 0, 2)
             op1(0)
             op1(1)
             op2(0)
             tr(0)
             op2(1)
             tr(1)
+            inter("S", e_t[0], e_raw[0], 0)
+            inter("V", e_t[0], e_raw[0], 1)
             tcopy("S", 0)
             tcopy("S", 1)
-            inter("S", eg_t, eg_raw, 0)
-            inter("S", eg_t, eg_raw, 1)
+            quant(ec[0], esc[0], e_t[0], 0, 256, E4M3)
+            quant(ec[0], esc[0], e_t[0], 256, 256, E4M3)
+            tq(0)
             op1(2)
             op1(3)
             op2(2)
             tr(2)
             op2(3)
             tr(3)
+            inter("S", eg_t, eg_raw, 0)
+            inter("S", eg_t, eg_raw, 1)
             d_inter("S", 0, 0)
-            tcopy("S", 2)
-            tcopy("S", 3)
-            tq(0)
-            inter("V", e_t[0], e_raw[0], 0)
+            d_inter("V", 0, 1)
             quant(egc, egs, eg_t, 0, N, E4M3)
             mm0(0)
-            mm0(1)
+            tcopy("S", 2)
             oc0("S", 0)
             st0(0)
+            tcopy("S", 3)
+            mm0(1)
             oc0("S", 1)
             st0(1)
+            quant(dc[0], dsc[0], d_t[0], 256, 256, E5M2)
+            mm1(0, 2)
+            mm1(0, 3)
             op1(4)
-            op1(5)
+            quant(dc[0], dsc[0], d_t[0], 0, 256, E5M2)
+            mm1(0, 0)
+            mm1(0, 1)
             op2(4)
             tr(4)
+            op1(5)
             tq(1)
-            op2(5)
-            tr(5)
             mm0(2)
             mm0(3)
-            tcopy("S", 4)
-            inter("S", e_t[0], e_raw[0], 1)
-            tcopy("S", 5)
+            op2(5)
+            tr(5)
             op1(6)
-            quant(dc[0], dsc[0], d_t[0], 0, 256, E5M2)
             op1(7)
             op2(6)
             tr(6)
-            quant(ec[0], esc[0], e_t[0], 0, 256, E4M3)
             op2(7)
             tr(7)
-            tq(2)
-            mm0(4)
-            quant(ec[0], esc[0], e_t[0], 256, 256, E4M3)
-            mm1(0, 0)
-            mm1(0, 1)
+            inter("S", e_t[1], e_raw[1], 0)
+            tcopy("S", 4)
             oc0("S", 2)
             st0(2)
+            tcopy("S", 5)
             oc0("S", 3)
             st0(3)
-            inter("S", e_t[1], e_raw[1], 0)
-            d_inter("V", 1, 0)
-            inter("V", e_t[1], e_raw[1], 1)
-            tcopy("S", 6)
+            tq(2)
+            mm0(4)
             mm0(5)
+            inter("V", e_t[1], e_raw[1], 1)
+            d_inter("V", 1, 0)
+            d_inter("S", 1, 1)
+            quant(ec[1], esc[1], e_t[1], 256, 256, E4M3)
+            quant(ec[1], esc[1], e_t[1], 0, 256, E4M3)
             quant(dc[1], dsc[1], d_t[1], 0, 256, E5M2)
-            tcopy("S", 7)
+            mm1(1, 0)
+            mm1(1, 1)
             oc0("S", 4)
             st0(4)
             oc0("S", 5)
             st0(5)
-            quant(ec[1], esc[1], e_t[1], 256, 256, E4M3)
-            quant(ec[1], esc[1], e_t[1], 0, 256, E4M3)
-            mm1(1, 0)
-            mm1(1, 1)
-            d_inter("V", 0, 1)
+            quant(dc[1], dsc[1], d_t[1], 256, 256, E5M2)
+            mm1(1, 2)
+            mm1(1, 3)
+            tcopy("V", 6)
+            tcopy("V", 7)
             tq(3)
             mm0(6)
             mm0(7)
             oc1("S", 0)
             st1(0)
-            d_inter("V", 1, 1)
-            oc0("S", 6)
-            st0(6)
-            oc0("S", 7)
-            st0(7)
-            quant(dc[0], dsc[0], d_t[0], 256, 256, E5M2)
-            quant(dc[1], dsc[1], d_t[1], 256, 256, E5M2)
-            mm1(0, 2)
-            mm1(1, 2)
-            mm1(0, 3)
-            mm1(1, 3)
-            oc1("V", 1)
+            oc1("S", 1)
             st1(1)
             oc1("S", 2)
             st1(2)
-            oc1("V", 3)
+            oc1("S", 3)
             st1(3)
+            oc0("V", 6)
+            st0(6)
+            oc0("S", 7)
+            st0(7)

@@ -162,93 +162,93 @@ def tile_bspncn_pb_v_kernel(tc, e_gen2, e_disc2, e_gen1, e_disc3, j2, v2, x2, Eg
             load_v(0, 1, 2)
             load_g_half(0, 0)
             load_e(0)
-            load_g(1, 0, 2)
             load_v(1, 0, 2)
+            load_g(1, 0, 2)
             nc.sync.dma_start(out=eg_raw[:], in_=eg_hbm)
             load_g(2, 0, 2)
             load_v(2, 0, 2)
             load_v(3, 0, 2)
-            load_e(1)
             load_g(3, 0, 2)
+            load_e(1)
             op1(0)
             op1(1)
             op2(0)
-            tr(0)
             op2(1)
+            tr(0)
             tr(1)
             inter("S", e_t[0], e_raw[0], 0)
-            inter("V", e_t[0], e_raw[0], 1)
             tcopy("S", 0)
             tcopy("S", 1)
             quant(ec[0], esc[0], e_t[0], 0, 256, E4M3)
-            quant(ec[0], esc[0], e_t[0], 256, 256, E4M3)
-            tq(0)
+            inter("S", e_t[0], e_raw[0], 1)
+            inter("S", eg_t, eg_raw, 0)
             op1(2)
             op1(3)
             op2(2)
-            tr(2)
             op2(3)
+            tr(2)
             tr(3)
-            inter("S", eg_t, eg_raw, 0)
-            inter("S", eg_t, eg_raw, 1)
+            inter("V", eg_t, eg_raw, 1)
             d_inter("S", 0, 0)
-            d_inter("V", 0, 1)
+            tq(0)
             quant(egc, egs, eg_t, 0, N, E4M3)
-            mm0(0)
-            tcopy("S", 2)
-            oc0("S", 0)
-            st0(0)
-            tcopy("S", 3)
-            mm0(1)
-            oc0("S", 1)
-            st0(1)
-            quant(dc[0], dsc[0], d_t[0], 256, 256, E5M2)
-            mm1(0, 2)
-            mm1(0, 3)
-            op1(4)
+            quant(ec[0], esc[0], e_t[0], 256, 256, E4M3)
             quant(dc[0], dsc[0], d_t[0], 0, 256, E5M2)
+            tcopy("S", 2)
+            tcopy("S", 3)
+            mm0(0)
+            mm0(1)
             mm1(0, 0)
             mm1(0, 1)
-            op2(4)
-            tr(4)
+            oc0("S", 0)
+            st0(0)
+            oc0("S", 1)
+            st0(1)
+            d_inter("S", 0, 1)
+            op1(4)
             op1(5)
-            tq(1)
-            mm0(2)
-            mm0(3)
+            op2(4)
             op2(5)
+            tr(4)
             tr(5)
             op1(6)
+            tcopy("S", 4)
+            tcopy("S", 5)
+            tq(1)
             op1(7)
+            mm0(2)
+            mm0(3)
+            oc0("S", 2)
+            st0(2)
+            oc0("S", 3)
+            st0(3)
             op2(6)
             tr(6)
             op2(7)
-            tr(7)
-            inter("S", e_t[1], e_raw[1], 0)
-            tcopy("S", 4)
-            oc0("S", 2)
-            st0(2)
-            tcopy("S", 5)
-            oc0("S", 3)
-            st0(3)
             tq(2)
             mm0(4)
             mm0(5)
+            tr(7)
+            inter("S", e_t[1], e_raw[1], 0)
             inter("V", e_t[1], e_raw[1], 1)
             d_inter("V", 1, 0)
-            d_inter("S", 1, 1)
             quant(ec[1], esc[1], e_t[1], 256, 256, E4M3)
-            quant(ec[1], esc[1], e_t[1], 0, 256, E4M3)
             quant(dc[1], dsc[1], d_t[1], 0, 256, E5M2)
+            quant(ec[1], esc[1], e_t[1], 0, 256, E4M3)
             mm1(1, 0)
             mm1(1, 1)
             oc0("S", 4)
             st0(4)
             oc0("S", 5)
             st0(5)
+            tcopy("S", 6)
+            d_inter("V", 1, 1)
+            quant(dc[0], dsc[0], d_t[0], 256, 256, E5M2)
             quant(dc[1], dsc[1], d_t[1], 256, 256, E5M2)
+            mm1(0, 2)
             mm1(1, 2)
+            mm1(0, 3)
             mm1(1, 3)
-            tcopy("V", 6)
             tcopy("V", 7)
             tq(3)
             mm0(6)
@@ -263,5 +263,5 @@ def tile_bspncn_pb_v_kernel(tc, e_gen2, e_disc2, e_gen1, e_disc3, j2, v2, x2, Eg
             st1(3)
             oc0("V", 6)
             st0(6)
-            oc0("S", 7)
+            oc0("V", 7)
             st0(7)

@@ -65,9 +65,6 @@ def tile_bspncn_pb_v_kernel(tc, e_gen2, e_disc2, e_gen1, e_disc3, j2, v2, x2, Eg
         def load_g(i, a, b):
             nc.sync.dma_start(out=g_t[i][:, a:b, :], in_=g_hbm[i // 2][:, 2 * (i % 2) + a:2 * (i % 2) + b, 0:2 * N])
 
-        def load_g_half(i, c0):
-            nc.sync.dma_start(out=g_t[i][:, :, c0:c0 + N], in_=g_hbm[i // 2][:, 2 * (i % 2):2 * (i % 2) + 2, c0:c0 + N])
-
         def load_e(g):
             nc.sync.dma_start(out=e_raw[g][:], in_=e_hbm[g])
 
@@ -139,8 +136,8 @@ def tile_bspncn_pb_v_kernel(tc, e_gen2, e_disc2, e_gen1, e_disc3, j2, v2, x2, Eg
         def oc0(eng, k):
             copy(eng, r0[k // 2][:, k % 2, :], o0s[k][:])
 
-        def st0(k):
-            nc.sync.dma_start(out=o0_hbm[k // 4][:, k % 4, :], in_=r0[k // 2][:, k % 2, :])
+        def st0(i):
+            nc.sync.dma_start(out=o0_hbm[i // 2][:, 2 * (i % 2):2 * (i % 2) + 2, :], in_=r0[i][:])
 
         o1 = [o1_psum.tile([P, N], F32, name=f"o1p{t}") for t in range(4)]
 
@@ -157,10 +154,10 @@ def tile_bspncn_pb_v_kernel(tc, e_gen2, e_disc2, e_gen1, e_disc3, j2, v2, x2, Eg
 
         make_identity(nc, ident[:])
         with tc.manual_schedule():
-            load_g_half(0, N)
+            load_g(0, 0, 1)
             load_v(0, 0, 1)
+            load_g(0, 1, 2)
             load_v(0, 1, 2)
-            load_g_half(0, 0)
             load_e(0)
             load_v(1, 0, 2)
             load_g(1, 0, 2)
@@ -201,9 +198,8 @@ def tile_bspncn_pb_v_kernel(tc, e_gen2, e_disc2, e_gen1, e_disc3, j2, v2, x2, Eg
             mm1(0, 0)
             mm1(0, 1)
             oc0("S", 0)
-            st0(0)
             oc0("S", 1)
-            st0(1)
+            st0(0)
             d_inter("S", 0, 1)
             op1(4)
             op1(5)
@@ -219,9 +215,8 @@ def tile_bspncn_pb_v_kernel(tc, e_gen2, e_disc2, e_gen1, e_disc3, j2, v2, x2, Eg
             mm0(2)
             mm0(3)
             oc0("S", 2)
-            st0(2)
             oc0("S", 3)
-            st0(3)
+            st0(1)
             op2(6)
             tr(6)
             op2(7)
@@ -238,9 +233,8 @@ def tile_bspncn_pb_v_kernel(tc, e_gen2, e_disc2, e_gen1, e_disc3, j2, v2, x2, Eg
             mm1(1, 0)
             mm1(1, 1)
             oc0("S", 4)
-            st0(4)
             oc0("S", 5)
-            st0(5)
+            st0(2)
             tcopy("S", 6)
             d_inter("V", 1, 1)
             quant(dc[0], dsc[0], d_t[0], 256, 256, E5M2)
@@ -262,6 +256,5 @@ def tile_bspncn_pb_v_kernel(tc, e_gen2, e_disc2, e_gen1, e_disc3, j2, v2, x2, Eg
             oc1("S", 3)
             st1(3)
             oc0("V", 6)
-            st0(6)
             oc0("V", 7)
-            st0(7)
+            st0(3)

@@ -139,6 +139,9 @@ def tile_bspncn_pb_v_kernel(tc, e_gen2, e_disc2, e_gen1, e_disc3, j2, v2, x2, Eg
         def st0(i):
             nc.sync.dma_start(out=o0_hbm[i // 2][:, 2 * (i % 2):2 * (i % 2) + 2, :], in_=r0[i][:])
 
+        def st0_unit(k):
+            nc.sync.dma_start(out=o0_hbm[k // 4][:, k % 4, :], in_=r0[k // 2][:, k % 2, :])
+
         o1 = [o1_psum.tile([P, N], F32, name=f"o1p{t}") for t in range(4)]
 
         def mm1(g, t):
@@ -159,17 +162,19 @@ def tile_bspncn_pb_v_kernel(tc, e_gen2, e_disc2, e_gen1, e_disc3, j2, v2, x2, Eg
             load_g(0, 1, 2)
             load_v(0, 1, 2)
             load_e(0)
+
             load_v(1, 0, 2)
             load_g(1, 0, 2)
             nc.sync.dma_start(out=eg_raw[:], in_=eg_hbm)
+
             load_g(2, 0, 2)
             load_v(2, 0, 2)
             load_v(3, 0, 2)
             load_g(3, 0, 2)
             load_e(1)
             op1(0)
-            op1(1)
             op2(0)
+            op1(1)
             op2(1)
             tr(0)
             tr(1)
@@ -233,8 +238,9 @@ def tile_bspncn_pb_v_kernel(tc, e_gen2, e_disc2, e_gen1, e_disc3, j2, v2, x2, Eg
             mm1(1, 0)
             mm1(1, 1)
             oc0("S", 4)
+            st0_unit(4)
             oc0("S", 5)
-            st0(2)
+            st0_unit(5)
             tcopy("S", 6)
             d_inter("V", 1, 1)
             quant(dc[0], dsc[0], d_t[0], 256, 256, E5M2)
@@ -256,5 +262,6 @@ def tile_bspncn_pb_v_kernel(tc, e_gen2, e_disc2, e_gen1, e_disc3, j2, v2, x2, Eg
             oc1("S", 3)
             st1(3)
             oc0("V", 6)
+            st0_unit(6)
             oc0("V", 7)
-            st0(3)
+            st0_unit(7)

from contextlib import ExitStack

import concourse.mybir as mybir
from concourse.masks import make_identity

F32 = mybir.dt.float32
BF16 = mybir.dt.bfloat16
U32 = mybir.dt.uint32
U8 = mybir.dt.uint8
E4M3 = mybir.dt.float8_e4m3fn_x4
E5M2 = mybir.dt.float8_e5m2_x4
OP = mybir.AluOpType
COPY = mybir.ActivationFunctionType.Copy

P = 128
PACK = 4
N = 512
TOKENS = 1024
FLOPS = 2 * 2 * TOKENS * N * N
BYTES = TOKENS * N * (4 + 2 + 2 + 2) + N * N * 2 + TOKENS * N * 4 + N * N * 4


def tile_bspncn_pb_v_kernel(tc, e_gen2, e_disc2, e_gen1, e_disc3, j2, v2, x2, Eg1, Ed2, v_pre, grad_out, out_0, out_1):
    nc = tc.nc
    v_hbm = v_pre.rearrange("(g p j) w -> g p j w", p=P, j=PACK)
    g_hbm = grad_out.rearrange("(g p j) w -> g p j w", p=P, j=PACK)
    e_hbm = e_gen1.rearrange("(g p j) w -> g p j w", p=P, j=PACK)
    eg_hbm = Eg1.rearrange("(p j) w -> p j w", j=PACK)
    o0_hbm = out_0.rearrange("(g p j) w -> g p j w", p=P, j=PACK)

    with ExitStack() as ctx:
        keep = ctx.enter_context(tc.tile_pool(name="keep", bufs=1))
        t_psum = ctx.enter_context(tc.psum_pool(name="t_psum", bufs=2))
        o0_psum = ctx.enter_context(tc.psum_pool(name="o0_psum", bufs=2))
        o1_psum = ctx.enter_context(tc.psum_pool(name="o1_psum", bufs=1))

        def sb(name, shape, dtype):
            return keep.tile(shape, dtype, name=name, align_bytes=64)

        ident = sb("ident", [P, P], F32)
        v_t = [sb(f"v{i}", [P, 2, N], F32) for i in range(4)]
        g_t = [sb(f"g{i}", [P, 2, 2 * N], BF16) for i in range(4)]
        e_raw = [sb(f"e{g}", [P, PACK, N], BF16) for g in range(2)]
        eg_raw = sb("eg", [P, PACK, N], BF16)
        m_t = [sb(f"m{k}", [P, N], BF16) for k in range(8)]
        s_t = [sb(f"s{g}", [P, PACK, N], F32) for g in range(2)]
        d_t = [sb(f"d{g}", [P, N, PACK], BF16) for g in range(2)]
        e_t = [sb(f"ei{g}", [P, N, PACK], BF16) for g in range(2)]
        eg_t = sb("egi", [P, N, PACK], BF16)
        x_t = [sb(f"x{i}", [P, 2, P, PACK], BF16) for i in range(4)]
        dc = [sb(f"dc{g}", [P, N], U32) for g in range(2)]
        dsc = [sb(f"ds{g}", [P, N], U8) for g in range(2)]
        ec = [sb(f"ec{g}", [P, N], U32) for g in range(2)]
        esc = [sb(f"es{g}", [P, N], U8) for g in range(2)]
        egc = sb("egc", [P, N], U32)
        egs = sb("egs", [P, N], U8)
        xc = [sb(f"xc{i}", [P, 2 * P], U32) for i in range(4)]
        xs = [sb(f"xs{i}", [P, 2 * P], U8) for i in range(4)]
        r0 = [sb(f"r0{i}", [P, 2, N], F32) for i in range(4)]
        r1 = [sb(f"r1{t}", [P, N], F32) for t in range(4)]

        def load_v(i, a, b):
            nc.sync.dma_start(out=v_t[i][:, a:b, :], in_=v_hbm[i // 2][:, 2 * (i % 2) + a:2 * (i % 2) + b, :])

        def load_g(i, a, b):
            nc.sync.dma_start(out=g_t[i][:, a:b, :], in_=g_hbm[i // 2][:, 2 * (i % 2) + a:2 * (i % 2) + b, 0:2 * N])

        def load_e(g):
            nc.sync.dma_start(out=e_raw[g][:], in_=e_hbm[g])

        def copy(eng, out, in_):
            if eng == "V":
                nc.vector.tensor_copy(out=out, in_=in_)
            else:
                nc.scalar.copy(out=out, in_=in_)

        def four_by_four_in(ap):
            return ap.rearrange("p j (c i) -> p c j i", i=4)

        def four_by_four_out(ap):
            return ap.rearrange("p (c i) j -> p c j i", i=4)

        def inter(eng, dst, src, h):
            c = slice(256 * h, 256 * h + 256)
            copy(eng, four_by_four_out(dst[:, c, :]), four_by_four_in(src[:, :, c]))

        def scale_round(eng, out, in_):
            if eng == "V":
                nc.vector.tensor_scalar(out=out, in0=in_, scalar1=0.1, scalar2=None, op0=OP.mult)
            else:
                nc.scalar.activation(out=out, in_=in_, func=COPY, scale=0.1)

        def d_inter(eng, g, h):
            c = slice(256 * h, 256 * h + 256)
            scale_round(eng, four_by_four_out(d_t[g][:, c, :]), four_by_four_in(s_t[g][:, :, c]))

        def quant(dst, sc, src, c0, w, fmt):
            nc.vector.quantize_mx(out=dst[:, c0:c0 + w].bitcast(fmt), scales=sc[:, c0:c0 + w],
                                  in_=src[:, c0:c0 + w, :].rearrange("p w j -> p (w j)"))

        def op1(k):
            i, jj = divmod(k, 2)
            nc.vector.scalar_tensor_tensor(out=m_t[k][:], in0=v_t[i][:, jj, :], scalar=0.4,
                                           in1=g_t[i][:, jj, N:2 * N], op0=OP.is_le, op1=OP.mult)

        def op2(k):
            i, jj = divmod(k, 2)
            nc.vector.scalar_tensor_tensor(out=s_t[k // 4][:, k % 4, :], in0=m_t[k][:], scalar=0.05,
                                           in1=g_t[i][:, jj, 0:N], op0=OP.mult, op1=OP.add)

        tps = {}

        def tr(k):
            tp = t_psum.tile([P, PACK, P], F32, name="tp")
            tps[k] = tp
            for t in range(PACK):
                nc.tensor.transpose(tp[:, t, :], s_t[k // 4][:, k % 4, t::PACK], ident[:])

        def tcopy(eng, k):
            scale_round(eng, x_t[k // 2][:, k % 2, :, :], tps[k][:].rearrange("q t p -> q p t"))

        def tq(i):
            nc.vector.quantize_mx(out=xc[i][:].bitcast(E5M2), scales=xs[i][:],
                                  in_=x_t[i][:].rearrange("q j p t -> q (j p t)"))

        o0s = {}

        def mm0(k):
            i, jj = divmod(k, 2)
            op = o0_psum.tile([P, N], F32, name="o0p")
            o0s[k] = op
            c = slice(P * jj, P * jj + P)
            nc.tensor.matmul_mx(out=op[:], lhsT=xc[i][:, c].bitcast(E5M2), lhsT_scale=xs[i][:, c],
                                rhs=egc[:].bitcast(E4M3), rhs_scale=egs[:], start=True, stop=True)

        def oc0(eng, k):
            copy(eng, r0[k // 2][:, k % 2, :], o0s[k][:])

        def st0(i):
            nc.sync.dma_start(out=o0_hbm[i // 2][:, 2 * (i % 2):2 * (i % 2) + 2, :], in_=r0[i][:])

        def st0_unit(k):
            nc.sync.dma_start(out=o0_hbm[k // 4][:, k % 4, :], in_=r0[k // 2][:, k % 2, :])

        o1 = [o1_psum.tile([P, N], F32, name=f"o1p{t}") for t in range(4)]

        def mm1(g, t):
            c = slice(P * t, P * t + P)
            nc.tensor.matmul_mx(out=o1[t][:], lhsT=dc[g][:, c].bitcast(E5M2), lhsT_scale=dsc[g][:, c],
                                rhs=ec[g][:].bitcast(E4M3), rhs_scale=esc[g][:], start=(g == 0), stop=(g == 1))

        def oc1(eng, t):
            copy(eng, r1[t][:], o1[t][:])

        def st1(t):
            nc.sync.dma_start(out=out_1[P * t:P * t + P, :], in_=r1[t][:])

        make_identity(nc, ident[:])
        with tc.manual_schedule():
            load_g(0, 0, 1)
            load_v(0, 0, 1)
            load_g(0, 1, 2)
            load_v(0, 1, 2)
            load_e(0)

            load_v(1, 0, 2)
            load_g(1, 0, 2)
            nc.sync.dma_start(out=eg_raw[:], in_=eg_hbm)

            load_g(2, 0, 2)
            load_v(2, 0, 2)
            load_v(3, 0, 2)
            load_g(3, 0, 2)
            load_e(1)
            op1(0)
            op2(0)
            op1(1)
            op2(1)
            tr(0)
            tr(1)
            inter("S", e_t[0], e_raw[0], 0)
            tcopy("S", 0)
            tcopy("S", 1)
            quant(ec[0], esc[0], e_t[0], 0, 256, E4M3)
            inter("S", e_t[0], e_raw[0], 1)
            inter("S", eg_t, eg_raw, 0)
            op1(2)
            op1(3)
            op2(2)
            op2(3)
            tr(2)
            tr(3)
            inter("V", eg_t, eg_raw, 1)
            d_inter("S", 0, 0)
            tq(0)
            quant(egc, egs, eg_t, 0, N, E4M3)
            quant(ec[0], esc[0], e_t[0], 256, 256, E4M3)
            quant(dc[0], dsc[0], d_t[0], 0, 256, E5M2)
            tcopy("S", 2)
            tcopy("S", 3)
            mm0(0)
            mm0(1)
            mm1(0, 0)
            mm1(0, 1)
            oc0("S", 0)
            oc0("S", 1)
            st0(0)
            d_inter("S", 0, 1)
            op1(4)
            op1(5)
            op2(4)
            op2(5)
            tr(4)
            tr(5)
            op1(6)
            tcopy("S", 4)
            tcopy("S", 5)
            tq(1)
            op1(7)
            mm0(2)
            mm0(3)
            oc0("S", 2)
            oc0("S", 3)
            st0(1)
            op2(6)
            tr(6)
            op2(7)
            tq(2)
            mm0(4)
            mm0(5)
            tr(7)
            inter("S", e_t[1], e_raw[1], 0)
            inter("V", e_t[1], e_raw[1], 1)
            d_inter("V", 1, 0)
            quant(ec[1], esc[1], e_t[1], 256, 256, E4M3)
            quant(dc[1], dsc[1], d_t[1], 0, 256, E5M2)
            quant(ec[1], esc[1], e_t[1], 0, 256, E4M3)
            mm1(1, 0)
            mm1(1, 1)
            oc0("S", 4)
            st0_unit(4)
            oc0("S", 5)
            st0_unit(5)
            tcopy("S", 6)
            d_inter("V", 1, 1)
            quant(dc[0], dsc[0], d_t[0], 256, 256, E5M2)
            quant(dc[1], dsc[1], d_t[1], 256, 256, E5M2)
            mm1(0, 2)
            mm1(1, 2)
            mm1(0, 3)
            mm1(1, 3)
            tcopy("V", 7)
            tq(3)
            mm0(6)
            mm0(7)
            oc1("S", 0)
            st1(0)
            oc1("S", 1)
            st1(1)
            oc1("S", 2)
            st1(2)
            oc1("S", 3)
            st1(3)
            oc0("V", 6)
            st0_unit(6)
            oc0("V", 7)
            st0_unit(7)
